import numpy as np
import ml_dtypes

BF16 = ml_dtypes.bfloat16


def bf(x):
    return np.asarray(x, np.float32).astype(BF16)


def f32(x):
    return np.asarray(x, np.float32)


def f64(x):
    return np.asarray(x).astype(np.float64)


def striped(idx):
    return np.tile(idx.reshape(-1, 16).T, (8, 1))


C, S, N = 512, 2048, 512


def sigmoid(v):
    return 1.0 / (1.0 + np.exp(-v))


def setup_inputs():
    return {"base": f32(np.random.standard_normal((C, S))), "x": bf(np.random.standard_normal((C, N))), "nb": bf(np.random.standard_normal((C, N))), "wv": bf(np.random.standard_normal((C, C)) / np.sqrt(C)), "wg": bf(np.random.standard_normal((2 * C, C)) / np.sqrt(2 * C)), "bg": f32(0.5 * np.random.standard_normal((C, 1))), "offs": striped(np.random.permutation(S)[:N])}


def reference(base, x, nb, wv, wg, bg, offs):
    idx = offs[:16].T.reshape(-1)
    ctx = f64(wv).T @ f64(nb)
    z = f64(wg)[:C].T @ ctx + f64(wg)[C:].T @ f64(x) + f64(bg)
    gate = sigmoid(z)
    out = f64(base).copy()
    out[:, idx] = gate * f64(x) + (1.0 - gate) * ctx
    return out

@@ -1,0 +1,84 @@
+import concourse.mybir as mybir
+
+P = 128
+C, S, N = 512, 2048, 512
+CB = C // P
+BF16, F32, U16 = mybir.dt.bfloat16, mybir.dt.float32, mybir.dt.uint16
+ADD, SUBTRACT, MULT = mybir.AluOpType.add, mybir.AluOpType.subtract, mybir.AluOpType.mult
+SIGMOID = mybir.ActivationFunctionType.Sigmoid
+
+FLOPS = 2 * C * N * (C + 2 * C)
+
+
+def block(b):
+    return slice(b * P, (b + 1) * P)
+
+
+def tile_gategatlayer_kernel(tc, base, x, nb, wv, wg, bg, offs, out):
+    nc = tc.nc
+    with (
+        tc.tile_pool(name="held", bufs=1) as held,
+        tc.psum_pool(name="psum", bufs=1) as psum,
+    ):
+        offsets = held.tile([P, N // 16], U16, name="offsets")
+        nc.sync.dma_start(offsets[:], offs)
+
+        nb_bf = [held.tile([P, N], BF16, name=f"nb_bf{k}") for k in range(CB)]
+        wv_bf = [held.tile([P, C], BF16, name=f"wv_bf{k}") for k in range(CB)]
+        x_bf = [held.tile([P, N], BF16, name=f"x_bf{k}") for k in range(CB)]
+        wg_x = [held.tile([P, C], BF16, name=f"wg_x{k}") for k in range(CB)]
+        wg_ctx = [held.tile([P, C], BF16, name=f"wg_ctx{k}") for k in range(CB)]
+        window = [held.tile([P, S], F32, name=f"window{b}") for b in range(CB)]
+        for k in range(CB):
+            nc.sync.dma_start(nb_bf[k][:], nb[block(k), :])
+            nc.scalar.dma_start(wv_bf[k][:], wv[block(k), :])
+        for k in range(CB):
+            nc.sync.dma_start(x_bf[k][:], x[block(k), :])
+            nc.scalar.dma_start(wg_x[k][:], wg[block(CB + k), :])
+        for k in range(CB):
+            nc.scalar.dma_start(wg_ctx[k][:], wg[block(k), :])
+        for b in range(CB):
+            nc.sync.dma_start(window[b][:], base[block(b), :])
+
+        bias = held.tile([P, CB], F32, name="bias")
+        with nc.allow_non_contiguous_dma(reason="512 biases, one to a partition and block"):
+            nc.gpsimd.dma_start(bias[:], bg.rearrange("(b p) o -> p (b o)", p=P))
+        neg_bias = held.tile([P, CB], F32, name="neg_bias")
+        nc.vector.tensor_scalar_mul(neg_bias[:], bias[:], -1.0)
+
+        x_f32 = [held.tile([P, N], F32, name=f"x_f32{b}") for b in range(CB)]
+        for b in range(CB):
+            nc.gpsimd.tensor_copy(x_f32[b][:], x_bf[b][:])
+
+        ctx_ps = [psum.tile([P, N], F32, name=f"ctx_ps{b}") for b in range(CB)]
+        for k in range(CB):
+            for b in range(CB):
+                nc.tensor.matmul(
+                    ctx_ps[b][:], wv_bf[k][:, block(b)], nb_bf[k][:], start=(k == 0), stop=(k == CB - 1)
+                )
+
+        ctx_bf = [held.tile([P, N], BF16, name=f"ctx_bf{b}") for b in range(CB)]
+        for b in range(CB):
+            if b % 2 == 0:
+                nc.scalar.copy(ctx_bf[b][:], ctx_ps[b][:])
+            else:
+                nc.vector.tensor_copy(ctx_bf[b][:], ctx_ps[b][:])
+        diff = [held.tile([P, N], F32, name=f"diff{b}") for b in range(CB)]
+        for b in range(CB):
+            nc.vector.tensor_tensor(diff[b][:], ctx_ps[b][:], x_bf[b][:], SUBTRACT)
+
+        for b in range(CB):
+            z_ps = psum.tile([P, N], F32, name=f"z_ps{b}")
+            for k in range(CB):
+                nc.tensor.matmul(z_ps[:], wg_x[k][:, block(b)], x_bf[k][:], start=(k == 0), stop=False)
+            for k in range(CB):
+                nc.tensor.matmul(z_ps[:], wg_ctx[k][:, block(b)], ctx_bf[k][:], start=False, stop=(k == CB - 1))
+
+            one_minus_gate = held.tile([P, N], F32, name=f"one_minus_gate{b}")
+            nc.scalar.activation(one_minus_gate[:], z_ps[:], SIGMOID, bias=neg_bias[:, b : b + 1], scale=-1.0)
+
+            shift = held.tile([P, N], F32, name=f"shift{b}")
+            nc.vector.tensor_tensor(shift[:], one_minus_gate[:], diff[b][:], MULT)
+
+            nc.vector.tensor_tensor(window[b][:].indirect(offsets[:]), x_f32[b][:], shift[:], ADD)
+            nc.sync.dma_start(out[block(b), :], window[b][:])

@@ -46,6 +46,10 @@ def tile_gategatlayer_kernel(tc, base, x, nb, wv, wg, bg, offs, out):
         neg_bias = held.tile([P, CB], F32, name="neg_bias")
         nc.vector.tensor_scalar_mul(neg_bias[:], bias[:], -1.0)
 
+        spare = held.tile([P, 1], F32, name="spare")
+        nc.vector.memset(spare[:], 0.0)
+        nc.scalar.activation(spare[:], spare[:], SIGMOID)
+
         x_f32 = [held.tile([P, N], F32, name=f"x_f32{b}") for b in range(CB)]
         for b in range(CB):
             nc.gpsimd.tensor_copy(x_f32[b][:], x_bf[b][:])
@@ -58,13 +62,9 @@ def tile_gategatlayer_kernel(tc, base, x, nb, wv, wg, bg, offs, out):
                 )
 
         ctx_bf = [held.tile([P, N], BF16, name=f"ctx_bf{b}") for b in range(CB)]
-        for b in range(CB):
-            if b % 2 == 0:
-                nc.scalar.copy(ctx_bf[b][:], ctx_ps[b][:])
-            else:
-                nc.vector.tensor_copy(ctx_bf[b][:], ctx_ps[b][:])
         diff = [held.tile([P, N], F32, name=f"diff{b}") for b in range(CB)]
         for b in range(CB):
+            nc.scalar.copy(ctx_bf[b][:], ctx_ps[b][:])
             nc.vector.tensor_tensor(diff[b][:], ctx_ps[b][:], x_bf[b][:], SUBTRACT)
 
         for b in range(CB):

@@ -20,31 +20,28 @@ def tile_gategatlayer_kernel(tc, base, x, nb, wv, wg, bg, offs, out):
         tc.tile_pool(name="held", bufs=1) as held,
         tc.psum_pool(name="psum", bufs=1) as psum,
     ):
+        nb_bf = held.tile([P, CB, N], BF16, name="nb_bf")
+        wv_bf = held.tile([P, CB, C], BF16, name="wv_bf")
+        x_bf = held.tile([P, CB, N], BF16, name="x_bf")
+        wg_x = held.tile([P, CB, C], BF16, name="wg_x")
+        wg_ctx = held.tile([P, CB, C], BF16, name="wg_ctx")
         offsets = held.tile([P, N // 16], U16, name="offsets")
-        nc.sync.dma_start(offsets[:], offs)
-
-        nb_bf = [held.tile([P, N], BF16, name=f"nb_bf{k}") for k in range(CB)]
-        wv_bf = [held.tile([P, C], BF16, name=f"wv_bf{k}") for k in range(CB)]
-        x_bf = [held.tile([P, N], BF16, name=f"x_bf{k}") for k in range(CB)]
-        wg_x = [held.tile([P, C], BF16, name=f"wg_x{k}") for k in range(CB)]
-        wg_ctx = [held.tile([P, C], BF16, name=f"wg_ctx{k}") for k in range(CB)]
         window = [held.tile([P, S], F32, name=f"window{b}") for b in range(CB)]
-        for k in range(CB):
-            nc.sync.dma_start(nb_bf[k][:], nb[block(k), :])
-            nc.scalar.dma_start(wv_bf[k][:], wv[block(k), :])
-        for k in range(CB):
-            nc.sync.dma_start(x_bf[k][:], x[block(k), :])
-            nc.scalar.dma_start(wg_x[k][:], wg[block(CB + k), :])
-        for k in range(CB):
-            nc.scalar.dma_start(wg_ctx[k][:], wg[block(k), :])
+        for k in range(2):
+            nc.sync.dma_start(nb_bf[:, k, :], nb[block(k), :])
+            nc.scalar.dma_start(wv_bf[:, k, :], wv[block(k), :])
+        nc.sync.dma_start(nb_bf[:, 2:, :], nb[2 * P :, :].rearrange("(k p) n -> p k n", p=P))
+        nc.scalar.dma_start(wv_bf[:, 2:, :], wv[2 * P :, :].rearrange("(k p) c -> p k c", p=P))
+        nc.sync.dma_start(x_bf[:], x.rearrange("(k p) n -> p k n", p=P))
+        nc.scalar.dma_start(wg_x[:], wg[C:, :].rearrange("(k p) c -> p k c", p=P))
+        nc.scalar.dma_start(wg_ctx[:], wg[:C, :].rearrange("(k p) c -> p k c", p=P))
+        nc.sync.dma_start(offsets[:], offs)
         for b in range(CB):
             nc.sync.dma_start(window[b][:], base[block(b), :])
 
         bias = held.tile([P, CB], F32, name="bias")
         with nc.allow_non_contiguous_dma(reason="512 biases, one to a partition and block"):
             nc.gpsimd.dma_start(bias[:], bg.rearrange("(b p) o -> p (b o)", p=P))
-        neg_bias = held.tile([P, CB], F32, name="neg_bias")
-        nc.vector.tensor_scalar_mul(neg_bias[:], bias[:], -1.0)
 
         spare = held.tile([P, 1], F32, name="spare")
         nc.vector.memset(spare[:], 0.0)
@@ -52,33 +49,33 @@ def tile_gategatlayer_kernel(tc, base, x, nb, wv, wg, bg, offs, out):
 
         x_f32 = [held.tile([P, N], F32, name=f"x_f32{b}") for b in range(CB)]
         for b in range(CB):
-            nc.gpsimd.tensor_copy(x_f32[b][:], x_bf[b][:])
+            nc.gpsimd.tensor_copy(x_f32[b][:], x_bf[:, b, :])
 
         ctx_ps = [psum.tile([P, N], F32, name=f"ctx_ps{b}") for b in range(CB)]
         for k in range(CB):
             for b in range(CB):
                 nc.tensor.matmul(
-                    ctx_ps[b][:], wv_bf[k][:, block(b)], nb_bf[k][:], start=(k == 0), stop=(k == CB - 1)
+                    ctx_ps[b][:], wv_bf[:, k, block(b)], nb_bf[:, k, :], start=(k == 0), stop=(k == CB - 1)
                 )
 
         ctx_bf = [held.tile([P, N], BF16, name=f"ctx_bf{b}") for b in range(CB)]
         diff = [held.tile([P, N], F32, name=f"diff{b}") for b in range(CB)]
         for b in range(CB):
             nc.scalar.copy(ctx_bf[b][:], ctx_ps[b][:])
-            nc.vector.tensor_tensor(diff[b][:], ctx_ps[b][:], x_bf[b][:], SUBTRACT)
+            nc.vector.tensor_tensor(diff[b][:], x_bf[:, b, :], ctx_ps[b][:], SUBTRACT)
 
         for b in range(CB):
             z_ps = psum.tile([P, N], F32, name=f"z_ps{b}")
             for k in range(CB):
-                nc.tensor.matmul(z_ps[:], wg_x[k][:, block(b)], x_bf[k][:], start=(k == 0), stop=False)
+                nc.tensor.matmul(z_ps[:], wg_x[:, k, block(b)], x_bf[:, k, :], start=(k == 0), stop=False)
             for k in range(CB):
-                nc.tensor.matmul(z_ps[:], wg_ctx[k][:, block(b)], ctx_bf[k][:], start=False, stop=(k == CB - 1))
+                nc.tensor.matmul(z_ps[:], wg_ctx[:, k, block(b)], ctx_bf[k][:], start=False, stop=(k == CB - 1))
 
-            one_minus_gate = held.tile([P, N], F32, name=f"one_minus_gate{b}")
-            nc.scalar.activation(one_minus_gate[:], z_ps[:], SIGMOID, bias=neg_bias[:, b : b + 1], scale=-1.0)
+            gate = held.tile([P, N], F32, name=f"gate{b}")
+            nc.scalar.activation(gate[:], z_ps[:], SIGMOID, bias=bias[:, b : b + 1])
 
             shift = held.tile([P, N], F32, name=f"shift{b}")
-            nc.vector.tensor_tensor(shift[:], one_minus_gate[:], diff[b][:], MULT)
+            nc.vector.scalar_tensor_tensor(shift[:], gate[:], 1.0, diff[b][:], SUBTRACT, MULT)
 
             nc.vector.tensor_tensor(window[b][:].indirect(offsets[:]), x_f32[b][:], shift[:], ADD)
             nc.sync.dma_start(out[block(b), :], window[b][:])

@@ -7,6 +7,8 @@ BF16, F32, U16 = mybir.dt.bfloat16, mybir.dt.float32, mybir.dt.uint16
 ADD, SUBTRACT, MULT = mybir.AluOpType.add, mybir.AluOpType.subtract, mybir.AluOpType.mult
 SIGMOID = mybir.ActivationFunctionType.Sigmoid
 
+WARM_MATMULS = 4
+
 FLOPS = 2 * C * N * (C + 2 * C)
 
 
@@ -34,24 +36,25 @@ def tile_gategatlayer_kernel(tc, base, x, nb, wv, wg, bg, offs, out):
         nc.scalar.dma_start(wv_bf[:, 2:, :], wv[2 * P :, :].rearrange("(k p) c -> p k c", p=P))
         nc.sync.dma_start(x_bf[:], x.rearrange("(k p) n -> p k n", p=P))
         nc.scalar.dma_start(wg_x[:], wg[C:, :].rearrange("(k p) c -> p k c", p=P))
-        nc.scalar.dma_start(wg_ctx[:], wg[:C, :].rearrange("(k p) c -> p k c", p=P))
+        nc.sync.dma_start(wg_ctx[:], wg[:C, :].rearrange("(k p) c -> p k c", p=P))
         nc.sync.dma_start(offsets[:], offs)
         for b in range(CB):
             nc.sync.dma_start(window[b][:], base[block(b), :])
 
         bias = held.tile([P, CB], F32, name="bias")
         with nc.allow_non_contiguous_dma(reason="512 biases, one to a partition and block"):
-            nc.gpsimd.dma_start(bias[:], bg.rearrange("(b p) o -> p (b o)", p=P))
+            nc.scalar.dma_start(bias[:], bg.rearrange("(b p) o -> p (b o)", p=P))
+
+        zeros = held.tile([P, N], BF16, name="zeros")
+        nc.vector.memset(zeros[:], 0.0)
 
         spare = held.tile([P, 1], F32, name="spare")
         nc.vector.memset(spare[:], 0.0)
         nc.scalar.activation(spare[:], spare[:], SIGMOID)
 
-        x_f32 = [held.tile([P, N], F32, name=f"x_f32{b}") for b in range(CB)]
-        for b in range(CB):
-            nc.gpsimd.tensor_copy(x_f32[b][:], x_bf[:, b, :])
-
         ctx_ps = [psum.tile([P, N], F32, name=f"ctx_ps{b}") for b in range(CB)]
+        for i in range(WARM_MATMULS):
+            nc.tensor.matmul(ctx_ps[0][:], zeros[:, :P], zeros[:], start=True, stop=True)
         for k in range(CB):
             for b in range(CB):
                 nc.tensor.matmul(
@@ -71,11 +74,14 @@ def tile_gategatlayer_kernel(tc, base, x, nb, wv, wg, bg, offs, out):
             for k in range(CB):
                 nc.tensor.matmul(z_ps[:], wg_ctx[:, k, block(b)], ctx_bf[k][:], start=False, stop=(k == CB - 1))
 
+            x_f32 = held.tile([P, N], F32, name=f"x_f32{b}")
+            nc.scalar.copy(x_f32[:], x_bf[:, b, :])
+
             gate = held.tile([P, N], F32, name=f"gate{b}")
             nc.scalar.activation(gate[:], z_ps[:], SIGMOID, bias=bias[:, b : b + 1])
 
             shift = held.tile([P, N], F32, name=f"shift{b}")
             nc.vector.scalar_tensor_tensor(shift[:], gate[:], 1.0, diff[b][:], SUBTRACT, MULT)
 
-            nc.vector.tensor_tensor(window[b][:].indirect(offsets[:]), x_f32[b][:], shift[:], ADD)
+            nc.vector.tensor_tensor(window[b][:].indirect(offsets[:]), x_f32[:], shift[:], ADD)
             nc.sync.dma_start(out[block(b), :], window[b][:])

@@ -16,6 +16,12 @@ def block(b):
     return slice(b * P, (b + 1) * P)
 
 
+def load_row_blocks(queue, tile, dram):
+    for k in range(2):
+        queue.dma_start(tile[:, k, :], dram[block(k), :])
+    queue.dma_start(tile[:, 2:, :], dram[2 * P :, :].rearrange("(k p) n -> p k n", p=P))
+
+
 def tile_gategatlayer_kernel(tc, base, x, nb, wv, wg, bg, offs, out):
     nc = tc.nc
     with (
@@ -29,14 +35,11 @@ def tile_gategatlayer_kernel(tc, base, x, nb, wv, wg, bg, offs, out):
         wg_ctx = held.tile([P, CB, C], BF16, name="wg_ctx")
         offsets = held.tile([P, N // 16], U16, name="offsets")
         window = [held.tile([P, S], F32, name=f"window{b}") for b in range(CB)]
-        for k in range(2):
-            nc.sync.dma_start(nb_bf[:, k, :], nb[block(k), :])
-            nc.scalar.dma_start(wv_bf[:, k, :], wv[block(k), :])
-        nc.sync.dma_start(nb_bf[:, 2:, :], nb[2 * P :, :].rearrange("(k p) n -> p k n", p=P))
-        nc.scalar.dma_start(wv_bf[:, 2:, :], wv[2 * P :, :].rearrange("(k p) c -> p k c", p=P))
-        nc.sync.dma_start(x_bf[:], x.rearrange("(k p) n -> p k n", p=P))
-        nc.scalar.dma_start(wg_x[:], wg[C:, :].rearrange("(k p) c -> p k c", p=P))
-        nc.sync.dma_start(wg_ctx[:], wg[:C, :].rearrange("(k p) c -> p k c", p=P))
+        load_row_blocks(nc.sync, nb_bf, nb)
+        load_row_blocks(nc.scalar, wv_bf, wv)
+        load_row_blocks(nc.sync, x_bf, x)
+        load_row_blocks(nc.scalar, wg_x, wg[C:, :])
+        load_row_blocks(nc.sync, wg_ctx, wg[:C, :])
         nc.sync.dma_start(offsets[:], offs)
         for b in range(CB):
             nc.sync.dma_start(window[b][:], base[block(b), :])
@@ -51,6 +54,10 @@ def tile_gategatlayer_kernel(tc, base, x, nb, wv, wg, bg, offs, out):
         spare = held.tile([P, 1], F32, name="spare")
         nc.vector.memset(spare[:], 0.0)
         nc.scalar.activation(spare[:], spare[:], SIGMOID)
+
+        x_f32 = [held.tile([P, N], F32, name=f"x_f32{b}") for b in range(CB)]
+        for b in range(CB):
+            nc.gpsimd.tensor_copy(x_f32[b][:], x_bf[:, b, :])
 
         ctx_ps = [psum.tile([P, N], F32, name=f"ctx_ps{b}") for b in range(CB)]
         for i in range(WARM_MATMULS):
@@ -74,14 +81,11 @@ def tile_gategatlayer_kernel(tc, base, x, nb, wv, wg, bg, offs, out):
             for k in range(CB):
                 nc.tensor.matmul(z_ps[:], wg_ctx[:, k, block(b)], ctx_bf[k][:], start=False, stop=(k == CB - 1))
 
-            x_f32 = held.tile([P, N], F32, name=f"x_f32{b}")
-            nc.scalar.copy(x_f32[:], x_bf[:, b, :])
-
             gate = held.tile([P, N], F32, name=f"gate{b}")
             nc.scalar.activation(gate[:], z_ps[:], SIGMOID, bias=bias[:, b : b + 1])
 
             shift = held.tile([P, N], F32, name=f"shift{b}")
             nc.vector.scalar_tensor_tensor(shift[:], gate[:], 1.0, diff[b][:], SUBTRACT, MULT)
 
-            nc.vector.tensor_tensor(window[b][:].indirect(offsets[:]), x_f32[:], shift[:], ADD)
+            nc.vector.tensor_tensor(window[b][:].indirect(offsets[:]), x_f32[b][:], shift[:], ADD)
             nc.sync.dma_start(out[block(b), :], window[b][:])

@@ -58,6 +58,8 @@ def tile_gategatlayer_kernel(tc, base, x, nb, wv, wg, bg, offs, out):
         x_f32 = [held.tile([P, N], F32, name=f"x_f32{b}") for b in range(CB)]
         for b in range(CB):
             nc.gpsimd.tensor_copy(x_f32[b][:], x_bf[:, b, :])
+        neg_bias = held.tile([P, CB], F32, name="neg_bias")
+        nc.gpsimd.tensor_scalar_mul(neg_bias[:], bias[:], -1.0)
 
         ctx_ps = [psum.tile([P, N], F32, name=f"ctx_ps{b}") for b in range(CB)]
         for i in range(WARM_MATMULS):
@@ -72,7 +74,7 @@ def tile_gategatlayer_kernel(tc, base, x, nb, wv, wg, bg, offs, out):
         diff = [held.tile([P, N], F32, name=f"diff{b}") for b in range(CB)]
         for b in range(CB):
             nc.scalar.copy(ctx_bf[b][:], ctx_ps[b][:])
-            nc.vector.tensor_tensor(diff[b][:], x_bf[:, b, :], ctx_ps[b][:], SUBTRACT)
+            nc.vector.tensor_tensor(diff[b][:], ctx_ps[b][:], x_bf[:, b, :], SUBTRACT)
 
         for b in range(CB):
             z_ps = psum.tile([P, N], F32, name=f"z_ps{b}")
@@ -81,11 +83,12 @@ def tile_gategatlayer_kernel(tc, base, x, nb, wv, wg, bg, offs, out):
             for k in range(CB):
                 nc.tensor.matmul(z_ps[:], wg_ctx[:, k, block(b)], ctx_bf[k][:], start=False, stop=(k == CB - 1))
 
-            gate = held.tile([P, N], F32, name=f"gate{b}")
-            nc.scalar.activation(gate[:], z_ps[:], SIGMOID, bias=bias[:, b : b + 1])
+            one_minus_gate = held.tile([P, N], F32, name=f"one_minus_gate{b}")
+            nc.scalar.activation(one_minus_gate[:], z_ps[:], SIGMOID, bias=neg_bias[:, b : b + 1], scale=-1.0)
 
             shift = held.tile([P, N], F32, name=f"shift{b}")
-            nc.vector.scalar_tensor_tensor(shift[:], gate[:], 1.0, diff[b][:], SUBTRACT, MULT)
+            product_engine = nc.vector if b == 0 else nc.gpsimd
+            product_engine.tensor_tensor(shift[:], one_minus_gate[:], diff[b][:], MULT)
 
             nc.vector.tensor_tensor(window[b][:].indirect(offsets[:]), x_f32[b][:], shift[:], ADD)
             nc.sync.dma_start(out[block(b), :], window[b][:])

@@ -57,9 +57,9 @@ def tile_gategatlayer_kernel(tc, base, x, nb, wv, wg, bg, offs, out):
 
         x_f32 = [held.tile([P, N], F32, name=f"x_f32{b}") for b in range(CB)]
         for b in range(CB):
-            nc.gpsimd.tensor_copy(x_f32[b][:], x_bf[:, b, :])
+            nc.vector.tensor_copy(x_f32[b][:], x_bf[:, b, :])
         neg_bias = held.tile([P, CB], F32, name="neg_bias")
-        nc.gpsimd.tensor_scalar_mul(neg_bias[:], bias[:], -1.0)
+        nc.vector.tensor_scalar_mul(neg_bias[:], bias[:], -1.0)
 
         ctx_ps = [psum.tile([P, N], F32, name=f"ctx_ps{b}") for b in range(CB)]
         for i in range(WARM_MATMULS):

@@ -12,14 +12,12 @@ WARM_MATMULS = 4
 FLOPS = 2 * C * N * (C + 2 * C)
 
 
+def by_partition(dram):
+    return dram.rearrange("(p b) n -> p b n", b=CB)
+
+
 def block(b):
-    return slice(b * P, (b + 1) * P)
-
-
-def load_row_blocks(queue, tile, dram):
-    for k in range(2):
-        queue.dma_start(tile[:, k, :], dram[block(k), :])
-    queue.dma_start(tile[:, 2:, :], dram[2 * P :, :].rearrange("(k p) n -> p k n", p=P))
+    return slice(b, C, CB)
 
 
 def tile_gategatlayer_kernel(tc, base, x, nb, wv, wg, bg, offs, out):
@@ -35,18 +33,19 @@ def tile_gategatlayer_kernel(tc, base, x, nb, wv, wg, bg, offs, out):
         wg_ctx = held.tile([P, CB, C], BF16, name="wg_ctx")
         offsets = held.tile([P, N // 16], U16, name="offsets")
         window = [held.tile([P, S], F32, name=f"window{b}") for b in range(CB)]
-        load_row_blocks(nc.sync, nb_bf, nb)
-        load_row_blocks(nc.scalar, wv_bf, wv)
-        load_row_blocks(nc.sync, x_bf, x)
-        load_row_blocks(nc.scalar, wg_x, wg[C:, :])
-        load_row_blocks(nc.sync, wg_ctx, wg[:C, :])
+        nc.sync.dma_start(nb_bf[:, :1, :], by_partition(nb)[:, :1, :])
+        nc.scalar.dma_start(wv_bf[:, :1, :], by_partition(wv)[:, :1, :])
+        nc.sync.dma_start(nb_bf[:, 1:, :], by_partition(nb)[:, 1:, :])
+        nc.scalar.dma_start(wv_bf[:, 1:, :], by_partition(wv)[:, 1:, :])
+        nc.sync.dma_start(x_bf[:], by_partition(x))
+        nc.scalar.dma_start(wg_x[:], by_partition(wg[C:, :]))
+        nc.sync.dma_start(wg_ctx[:], by_partition(wg[:C, :]))
         nc.sync.dma_start(offsets[:], offs)
         for b in range(CB):
-            nc.sync.dma_start(window[b][:], base[block(b), :])
+            nc.sync.dma_start(window[b][:], by_partition(base)[:, b, :])
 
         bias = held.tile([P, CB], F32, name="bias")
-        with nc.allow_non_contiguous_dma(reason="512 biases, one to a partition and block"):
-            nc.scalar.dma_start(bias[:], bg.rearrange("(b p) o -> p (b o)", p=P))
+        nc.scalar.dma_start(bias[:], bg.rearrange("(p b) o -> p (b o)", b=CB))
 
         zeros = held.tile([P, N], BF16, name="zeros")
         nc.vector.memset(zeros[:], 0.0)
@@ -91,4 +90,4 @@ def tile_gategatlayer_kernel(tc, base, x, nb, wv, wg, bg, offs, out):
             product_engine.tensor_tensor(shift[:], one_minus_gate[:], diff[b][:], MULT)
 
             nc.vector.tensor_tensor(window[b][:].indirect(offsets[:]), x_f32[b][:], shift[:], ADD)
-            nc.sync.dma_start(out[block(b), :], window[b][:])
+            nc.sync.dma_start(by_partition(out)[:, b, :], window[b][:])

@@ -3,6 +3,7 @@ import concourse.mybir as mybir
 P = 128
 C, S, N = 512, 2048, 512
 CB = C // P
+H = N // 2
 BF16, F32, U16 = mybir.dt.bfloat16, mybir.dt.float32, mybir.dt.uint16
 ADD, SUBTRACT, MULT = mybir.AluOpType.add, mybir.AluOpType.subtract, mybir.AluOpType.mult
 SIGMOID = mybir.ActivationFunctionType.Sigmoid
@@ -20,11 +21,16 @@ def block(b):
     return slice(b, C, CB)
 
 
+def half(h):
+    return slice(h * H, (h + 1) * H)
+
+
 def tile_gategatlayer_kernel(tc, base, x, nb, wv, wg, bg, offs, out):
     nc = tc.nc
     with (
         tc.tile_pool(name="held", bufs=1) as held,
         tc.psum_pool(name="psum", bufs=1) as psum,
+        tc.psum_pool(name="z_banks", bufs=4) as z_banks,
     ):
         nb_bf = held.tile([P, CB, N], BF16, name="nb_bf")
         wv_bf = held.tile([P, CB, C], BF16, name="wv_bf")
@@ -33,10 +39,9 @@ def tile_gategatlayer_kernel(tc, base, x, nb, wv, wg, bg, offs, out):
         wg_ctx = held.tile([P, CB, C], BF16, name="wg_ctx")
         offsets = held.tile([P, N // 16], U16, name="offsets")
         window = [held.tile([P, S], F32, name=f"window{b}") for b in range(CB)]
-        nc.sync.dma_start(nb_bf[:, :1, :], by_partition(nb)[:, :1, :])
-        nc.scalar.dma_start(wv_bf[:, :1, :], by_partition(wv)[:, :1, :])
-        nc.sync.dma_start(nb_bf[:, 1:, :], by_partition(nb)[:, 1:, :])
-        nc.scalar.dma_start(wv_bf[:, 1:, :], by_partition(wv)[:, 1:, :])
+        for blocks in (slice(0, 1), slice(1, 2), slice(2, CB)):
+            nc.sync.dma_start(nb_bf[:, blocks, :], by_partition(nb)[:, blocks, :])
+            nc.scalar.dma_start(wv_bf[:, blocks, :], by_partition(wv)[:, blocks, :])
         nc.sync.dma_start(x_bf[:], by_partition(x))
         nc.scalar.dma_start(wg_x[:], by_partition(wg[C:, :]))
         nc.sync.dma_start(wg_ctx[:], by_partition(wg[:C, :]))
@@ -63,11 +68,12 @@ def tile_gategatlayer_kernel(tc, base, x, nb, wv, wg, bg, offs, out):
         ctx_ps = [psum.tile([P, N], F32, name=f"ctx_ps{b}") for b in range(CB)]
         for i in range(WARM_MATMULS):
             nc.tensor.matmul(ctx_ps[0][:], zeros[:, :P], zeros[:], start=True, stop=True)
-        for k in range(CB):
+        for k in range(CB // 2):
             for b in range(CB):
-                nc.tensor.matmul(
-                    ctx_ps[b][:], wv_bf[:, k, block(b)], nb_bf[:, k, :], start=(k == 0), stop=(k == CB - 1)
-                )
+                nc.tensor.matmul(ctx_ps[b][:], wv_bf[:, k, block(b)], nb_bf[:, k, :], start=(k == 0), stop=False)
+        for b in range(CB):
+            for k in range(CB // 2, CB):
+                nc.tensor.matmul(ctx_ps[b][:], wv_bf[:, k, block(b)], nb_bf[:, k, :], start=False, stop=(k == CB - 1))
 
         ctx_bf = [held.tile([P, N], BF16, name=f"ctx_bf{b}") for b in range(CB)]
         diff = [held.tile([P, N], F32, name=f"diff{b}") for b in range(CB)]
@@ -76,18 +82,22 @@ def tile_gategatlayer_kernel(tc, base, x, nb, wv, wg, bg, offs, out):
             nc.vector.tensor_tensor(diff[b][:], ctx_ps[b][:], x_bf[:, b, :], SUBTRACT)
 
         for b in range(CB):
-            z_ps = psum.tile([P, N], F32, name=f"z_ps{b}")
-            for k in range(CB):
-                nc.tensor.matmul(z_ps[:], wg_x[:, k, block(b)], x_bf[:, k, :], start=(k == 0), stop=False)
-            for k in range(CB):
-                nc.tensor.matmul(z_ps[:], wg_ctx[:, k, block(b)], ctx_bf[k][:], start=False, stop=(k == CB - 1))
-
+            z_ps = [z_banks.tile([P, H], F32, name="z_ps") for h in range(2)]
             one_minus_gate = held.tile([P, N], F32, name=f"one_minus_gate{b}")
-            nc.scalar.activation(one_minus_gate[:], z_ps[:], SIGMOID, bias=neg_bias[:, b : b + 1], scale=-1.0)
-
             shift = held.tile([P, N], F32, name=f"shift{b}")
             product_engine = nc.vector if b == 0 else nc.gpsimd
-            product_engine.tensor_tensor(shift[:], one_minus_gate[:], diff[b][:], MULT)
+            for h in range(2):
+                for k in range(CB):
+                    nc.tensor.matmul(z_ps[h][:], wg_x[:, k, block(b)], x_bf[:, k, half(h)], start=(k == 0), stop=False)
+            for h in range(2):
+                for k in range(CB):
+                    nc.tensor.matmul(
+                        z_ps[h][:], wg_ctx[:, k, block(b)], ctx_bf[k][:, half(h)], start=False, stop=(k == CB - 1)
+                    )
+                nc.scalar.activation(
+                    one_minus_gate[:, half(h)], z_ps[h][:], SIGMOID, bias=neg_bias[:, b : b + 1], scale=-1.0
+                )
+                product_engine.tensor_tensor(shift[:, half(h)], one_minus_gate[:, half(h)], diff[b][:, half(h)], MULT)
 
             nc.vector.tensor_tensor(window[b][:].indirect(offsets[:]), x_f32[b][:], shift[:], ADD)
             nc.sync.dma_start(by_partition(out)[:, b, :], window[b][:])

@@ -85,7 +85,7 @@ def tile_gategatlayer_kernel(tc, base, x, nb, wv, wg, bg, offs, out):
             z_ps = [z_banks.tile([P, H], F32, name="z_ps") for h in range(2)]
             one_minus_gate = held.tile([P, N], F32, name=f"one_minus_gate{b}")
             shift = held.tile([P, N], F32, name=f"shift{b}")
-            product_engine = nc.vector if b == 0 else nc.gpsimd
+            product_engine = nc.vector if b <= 1 else nc.gpsimd
             for h in range(2):
                 for k in range(CB):
                     nc.tensor.matmul(z_ps[h][:], wg_x[:, k, block(b)], x_bf[:, k, half(h)], start=(k == 0), stop=False)

@@ -8,7 +8,7 @@ BF16, F32, U16 = mybir.dt.bfloat16, mybir.dt.float32, mybir.dt.uint16
 ADD, SUBTRACT, MULT = mybir.AluOpType.add, mybir.AluOpType.subtract, mybir.AluOpType.mult
 SIGMOID = mybir.ActivationFunctionType.Sigmoid
 
-WARM_MATMULS = 4
+WARM_MATMULS = 3
 
 FLOPS = 2 * C * N * (C + 2 * C)
 
@@ -19,10 +19,6 @@ def by_partition(dram):
 
 def block(b):
     return slice(b, C, CB)
-
-
-def half(h):
-    return slice(h * H, (h + 1) * H)
 
 
 def tile_gategatlayer_kernel(tc, base, x, nb, wv, wg, bg, offs, out):
@@ -82,22 +78,29 @@ def tile_gategatlayer_kernel(tc, base, x, nb, wv, wg, bg, offs, out):
             nc.vector.tensor_tensor(diff[b][:], ctx_ps[b][:], x_bf[:, b, :], SUBTRACT)
 
         for b in range(CB):
-            z_ps = [z_banks.tile([P, H], F32, name="z_ps") for h in range(2)]
+            pieces = [slice(0, H), slice(H, N)] if b == 0 else [slice(0, N)]
             one_minus_gate = held.tile([P, N], F32, name=f"one_minus_gate{b}")
             shift = held.tile([P, N], F32, name=f"shift{b}")
             product_engine = nc.vector if b <= 1 else nc.gpsimd
-            for h in range(2):
+            z_ps = [z_banks.tile([P, N], F32, name="z_ps") for piece in pieces]
+            for bank, piece in zip(z_ps, pieces):
+                z = bank[:, : piece.stop - piece.start]
                 for k in range(CB):
-                    nc.tensor.matmul(z_ps[h][:], wg_x[:, k, block(b)], x_bf[:, k, half(h)], start=(k == 0), stop=False)
-            for h in range(2):
+                    nc.tensor.matmul(z, wg_x[:, k, block(b)], x_bf[:, k, piece], start=(k == 0), stop=False)
+            for bank, piece in zip(z_ps, pieces):
+                z = bank[:, : piece.stop - piece.start]
                 for k in range(CB):
-                    nc.tensor.matmul(
-                        z_ps[h][:], wg_ctx[:, k, block(b)], ctx_bf[k][:, half(h)], start=False, stop=(k == CB - 1)
+                    nc.tensor.matmul(z, wg_ctx[:, k, block(b)], ctx_bf[k][:, piece], start=False, stop=(k == CB - 1))
+                for left in range(piece.start, piece.stop, H):
+                    part = slice(left, left + H)
+                    nc.scalar.activation(
+                        one_minus_gate[:, part],
+                        bank[:, left - piece.start : left - piece.start + H],
+                        SIGMOID,
+                        bias=neg_bias[:, b : b + 1],
+                        scale=-1.0,
                     )
-                nc.scalar.activation(
-                    one_minus_gate[:, half(h)], z_ps[h][:], SIGMOID, bias=neg_bias[:, b : b + 1], scale=-1.0
-                )
-                product_engine.tensor_tensor(shift[:, half(h)], one_minus_gate[:, half(h)], diff[b][:, half(h)], MULT)
+                    product_engine.tensor_tensor(shift[:, part], one_minus_gate[:, part], diff[b][:, part], MULT)
 
             nc.vector.tensor_tensor(window[b][:].indirect(offsets[:]), x_f32[b][:], shift[:], ADD)
             nc.sync.dma_start(by_partition(out)[:, b, :], window[b][:])

@@ -38,9 +38,11 @@ def tile_gategatlayer_kernel(tc, base, x, nb, wv, wg, bg, offs, out):
         for blocks in (slice(0, 1), slice(1, 2), slice(2, CB)):
             nc.sync.dma_start(nb_bf[:, blocks, :], by_partition(nb)[:, blocks, :])
             nc.scalar.dma_start(wv_bf[:, blocks, :], by_partition(wv)[:, blocks, :])
-        nc.sync.dma_start(x_bf[:], by_partition(x))
-        nc.scalar.dma_start(wg_x[:], by_partition(wg[C:, :]))
-        nc.sync.dma_start(wg_ctx[:], by_partition(wg[:C, :]))
+        for blocks in (slice(0, 2), slice(2, CB)):
+            nc.sync.dma_start(x_bf[:, blocks, :], by_partition(x)[:, blocks, :])
+            nc.scalar.dma_start(wg_x[:, blocks, :], by_partition(wg[C:, :])[:, blocks, :])
+        for blocks in (slice(0, 2), slice(2, CB)):
+            nc.sync.dma_start(wg_ctx[:, blocks, :], by_partition(wg[:C, :])[:, blocks, :])
         nc.sync.dma_start(offsets[:], offs)
         for b in range(CB):
             nc.sync.dma_start(window[b][:], by_partition(base)[:, b, :])
@@ -83,9 +85,9 @@ def tile_gategatlayer_kernel(tc, base, x, nb, wv, wg, bg, offs, out):
             shift = held.tile([P, N], F32, name=f"shift{b}")
             product_engine = nc.vector if b <= 1 else nc.gpsimd
             z_ps = [z_banks.tile([P, N], F32, name="z_ps") for piece in pieces]
-            for bank, piece in zip(z_ps, pieces):
-                z = bank[:, : piece.stop - piece.start]
-                for k in range(CB):
+            for k in range(CB):
+                for bank, piece in zip(z_ps, pieces):
+                    z = bank[:, : piece.stop - piece.start]
                     nc.tensor.matmul(z, wg_x[:, k, block(b)], x_bf[:, k, piece], start=(k == 0), stop=False)
             for bank, piece in zip(z_ps, pieces):
                 z = bank[:, : piece.stop - piece.start]

import concourse.mybir as mybir

P = 128
C, S, N = 512, 2048, 512
CB = C // P
H = N // 2
BF16, F32, U16 = mybir.dt.bfloat16, mybir.dt.float32, mybir.dt.uint16
ADD, SUBTRACT, MULT = mybir.AluOpType.add, mybir.AluOpType.subtract, mybir.AluOpType.mult
SIGMOID = mybir.ActivationFunctionType.Sigmoid

WARM_MATMULS = 3

FLOPS = 2 * C * N * (C + 2 * C)


def by_partition(dram):
    return dram.rearrange("(p b) n -> p b n", b=CB)


def block(b):
    return slice(b, C, CB)


def tile_gategatlayer_kernel(tc, base, x, nb, wv, wg, bg, offs, out):
    nc = tc.nc
    with (
        tc.tile_pool(name="held", bufs=1) as held,
        tc.psum_pool(name="psum", bufs=1) as psum,
        tc.psum_pool(name="z_banks", bufs=4) as z_banks,
    ):
        nb_bf = held.tile([P, CB, N], BF16, name="nb_bf")
        wv_bf = held.tile([P, CB, C], BF16, name="wv_bf")
        x_bf = held.tile([P, CB, N], BF16, name="x_bf")
        wg_x = held.tile([P, CB, C], BF16, name="wg_x")
        wg_ctx = held.tile([P, CB, C], BF16, name="wg_ctx")
        offsets = held.tile([P, N // 16], U16, name="offsets")
        window = [held.tile([P, S], F32, name=f"window{b}") for b in range(CB)]
        for blocks in (slice(0, 1), slice(1, 2), slice(2, CB)):
            nc.sync.dma_start(nb_bf[:, blocks, :], by_partition(nb)[:, blocks, :])
            nc.scalar.dma_start(wv_bf[:, blocks, :], by_partition(wv)[:, blocks, :])
        for blocks in (slice(0, 2), slice(2, CB)):
            nc.sync.dma_start(x_bf[:, blocks, :], by_partition(x)[:, blocks, :])
            nc.scalar.dma_start(wg_x[:, blocks, :], by_partition(wg[C:, :])[:, blocks, :])
        for blocks in (slice(0, 2), slice(2, CB)):
            nc.sync.dma_start(wg_ctx[:, blocks, :], by_partition(wg[:C, :])[:, blocks, :])
        nc.sync.dma_start(offsets[:], offs)
        for b in range(CB):
            nc.sync.dma_start(window[b][:], by_partition(base)[:, b, :])

        bias = held.tile([P, CB], F32, name="bias")
        nc.scalar.dma_start(bias[:], bg.rearrange("(p b) o -> p (b o)", b=CB))

        zeros = held.tile([P, N], BF16, name="zeros")
        nc.vector.memset(zeros[:], 0.0)

        spare = held.tile([P, 1], F32, name="spare")
        nc.vector.memset(spare[:], 0.0)
        nc.scalar.activation(spare[:], spare[:], SIGMOID)

        x_f32 = [held.tile([P, N], F32, name=f"x_f32{b}") for b in range(CB)]
        for b in range(CB):
            nc.vector.tensor_copy(x_f32[b][:], x_bf[:, b, :])
        neg_bias = held.tile([P, CB], F32, name="neg_bias")
        nc.vector.tensor_scalar_mul(neg_bias[:], bias[:], -1.0)

        ctx_ps = [psum.tile([P, N], F32, name=f"ctx_ps{b}") for b in range(CB)]
        for i in range(WARM_MATMULS):
            nc.tensor.matmul(ctx_ps[0][:], zeros[:, :P], zeros[:], start=True, stop=True)
        for k in range(CB // 2):
            for b in range(CB):
                nc.tensor.matmul(ctx_ps[b][:], wv_bf[:, k, block(b)], nb_bf[:, k, :], start=(k == 0), stop=False)
        for b in range(CB):
            for k in range(CB // 2, CB):
                nc.tensor.matmul(ctx_ps[b][:], wv_bf[:, k, block(b)], nb_bf[:, k, :], start=False, stop=(k == CB - 1))

        ctx_bf = [held.tile([P, N], BF16, name=f"ctx_bf{b}") for b in range(CB)]
        diff = [held.tile([P, N], F32, name=f"diff{b}") for b in range(CB)]
        for b in range(CB):
            nc.scalar.copy(ctx_bf[b][:], ctx_ps[b][:])
            nc.vector.tensor_tensor(diff[b][:], ctx_ps[b][:], x_bf[:, b, :], SUBTRACT)

        for b in range(CB):
            pieces = [slice(0, H), slice(H, N)] if b == 0 else [slice(0, N)]
            one_minus_gate = held.tile([P, N], F32, name=f"one_minus_gate{b}")
            shift = held.tile([P, N], F32, name=f"shift{b}")
            product_engine = nc.vector if b <= 1 else nc.gpsimd
            z_ps = [z_banks.tile([P, N], F32, name="z_ps") for piece in pieces]
            for k in range(CB):
                for bank, piece in zip(z_ps, pieces):
                    z = bank[:, : piece.stop - piece.start]
                    nc.tensor.matmul(z, wg_x[:, k, block(b)], x_bf[:, k, piece], start=(k == 0), stop=False)
            for bank, piece in zip(z_ps, pieces):
                z = bank[:, : piece.stop - piece.start]
                for k in range(CB):
                    nc.tensor.matmul(z, wg_ctx[:, k, block(b)], ctx_bf[k][:, piece], start=False, stop=(k == CB - 1))
                for left in range(piece.start, piece.stop, H):
                    part = slice(left, left + H)
                    nc.scalar.activation(
                        one_minus_gate[:, part],
                        bank[:, left - piece.start : left - piece.start + H],
                        SIGMOID,
                        bias=neg_bias[:, b : b + 1],
                        scale=-1.0,
                    )
                    product_engine.tensor_tensor(shift[:, part], one_minus_gate[:, part], diff[b][:, part], MULT)

            nc.vector.tensor_tensor(window[b][:].indirect(offsets[:]), x_f32[b][:], shift[:], ADD)
            nc.sync.dma_start(by_partition(out)[:, b, :], window[b][:])
